import numpy as np
import ml_dtypes


def mxq(x, axis, fmt="e4m3"):
    dtype, down = {"e4m3": (ml_dtypes.float8_e4m3fn, 7), "e5m2": (ml_dtypes.float8_e5m2, 14)}[fmt]
    v = np.moveaxis(np.asarray(x, np.float32).astype(ml_dtypes.bfloat16).astype(np.float64), axis, -1)
    blocks = v.reshape(v.shape[:-1] + (-1, 32))
    amax = np.abs(blocks).max(-1, keepdims=True)
    byte = np.maximum(np.where(amax > 0, np.frexp(amax)[1] - 1 + 127, 0) - down, 1)
    scale = np.exp2(byte - 127.0)
    codes = (blocks / scale).astype(np.float32).astype(dtype).astype(np.float64)
    return np.moveaxis((codes * scale).reshape(v.shape), -1, axis)


WIDE = False


def mx_kscale(k):
    if not WIDE:
        return np.ones(k)
    levels = np.array([10, -10, 5, -5, 0])
    a = np.random.permutation(np.resize(levels, k // 512 * 4)).reshape(k // 512, 4)
    idx = np.arange(k)
    return np.exp2(a[idx // 512, idx % 128 // 32])


BF16 = ml_dtypes.bfloat16


def bf(x):
    return np.asarray(x, np.float32).astype(BF16)


def f64(x):
    return np.asarray(x).astype(np.float64)


E2M1 = np.array([0.0, 0.5, 1.0, 1.5, 2.0, 3.0, 4.0, 6.0, -0.0, -0.5, -1.0, -1.5, -2.0, -3.0, -4.0, -6.0])


def pack_weight(w, fmt):
    k, n = w.shape
    w = f64(bf(w)).reshape(k // 32, 32, n)
    amax = np.abs(w).max(1)
    if fmt == "e4m3":
        byte = np.frexp(amax)[1] - 1 + 127 - 7
    else:
        mant, ex = np.frexp(amax / 6.0)
        byte = np.where(mant > 0.5, ex, ex - 1) + 127
    byte = np.clip(np.where(amax > 0, byte, 1), 1, 254)
    scaled = (w * np.exp2(127.0 - byte)[:, None, :]).reshape(k, n).astype(np.float32)
    by_word = np.ascontiguousarray(scaled.reshape(k // 512, 128, 4, n).transpose(0, 1, 3, 2))
    if fmt == "e4m3":
        words = by_word.astype(ml_dtypes.float8_e4m3fn).view(np.uint8)
    else:
        c = by_word.astype(ml_dtypes.float4_e2m1fn).view(np.uint8) & 0xF
        words = c[..., 0::2] | (c[..., 1::2] << 4)
    return np.ascontiguousarray(words), np.ascontiguousarray(byte.astype(np.uint8).reshape(k // 512, 16, n))


def unpack_weight(words, scales, fmt):
    g, p, n, _ = words.shape
    if fmt == "e4m3":
        vals = np.ascontiguousarray(words).view(ml_dtypes.float8_e4m3fn).astype(np.float64)
    else:
        nib = np.empty((g, p, n, 4), np.uint8)
        nib[..., 0::2] = words & 0xF
        nib[..., 1::2] = words >> 4
        vals = E2M1[nib]
    vals = vals * np.repeat(np.exp2(scales.astype(np.float64) - 127.0), 8, axis=1)[..., None]
    return vals.transpose(0, 1, 3, 2).reshape(g * 512, n)

def pack4(w):
    words, scales = pack_weight(w, "e2m1")
    return words.reshape(words.shape[0], 128, -1), scales


def unpack4(words, scales):
    return unpack_weight(words.reshape(words.shape[0], 128, -1, 2), scales, "e2m1")


B, N, D, H, DK, DV = 4, 1024, 512, 8, 64, 64


def xnorm(x, g):
    n = np.sqrt(np.sum(x * x, axis=-1, keepdims=True))
    return x * g / n


def setup_inputs():
    s = mx_kscale(D)
    queries = bf(np.random.standard_normal((B, N, D)) * s)
    Wq_words, Wq_scales = pack4(np.random.standard_normal((D, H * DK)) / np.sqrt(D) / s[:, None])
    return {
        "queries": queries,
        "Wq_words": Wq_words,
        "Wq_scales": Wq_scales,
        "bq": bf(np.random.standard_normal(H * DK) * 0.1),
        "gamma": bf(np.random.standard_normal((1, H, 1, 1)) * 2.0),
    }


def reference(queries, Wq_words, Wq_scales, bq, gamma):
    q = ((mxq(f64(queries), 2, "e4m3") @ unpack4(Wq_words, Wq_scales)) + f64(bq)).reshape(B, N, H, DK)
    return xnorm(q.transpose(0, 2, 1, 3), f64(gamma))

@@ -1,0 +1,231 @@
+from contextlib import ExitStack
+
+import concourse.mybir as mybir
+from concourse.masks import make_identity
+
+F32 = mybir.dt.float32
+BF16 = mybir.dt.bfloat16
+I32 = mybir.dt.int32
+U32 = mybir.dt.uint32
+U8 = mybir.dt.uint8
+FP8X4 = mybir.dt.float8_e4m3fn_x4
+FP4X4 = mybir.dt.float4_e2m1fn_x4
+ADD = mybir.AluOpType.add
+MULT = mybir.AluOpType.mult
+SQUARE = mybir.ActivationFunctionType.Square
+
+P = 128
+BATCH, TOKENS, D_IN = 4, 1024, 512
+HEADS, D_HEAD = 8, 64
+D_OUT = HEADS * D_HEAD
+TILES = 4
+BLOCK = P * TILES
+BLOCKS_PER_BATCH = TOKENS // BLOCK
+N_BLOCKS = BATCH * BLOCKS_PER_BATCH
+WORDS = D_IN // 2
+HEAD_SPLIT = 2
+GAIN_PAD = 32
+
+FLOPS = 2 * BATCH * TOKENS * D_IN * D_OUT
+
+
+def tile_ufoattention_pb_kernel(tc, queries, Wq_words, Wq_scales, bq, gamma, out):
+    nc = tc.nc
+    with ExitStack() as ctx:
+        ctx.enter_context(tc.manual_schedule())
+        consts = ctx.enter_context(tc.tile_pool(name="consts", bufs=1))
+        x_pool = ctx.enter_context(tc.tile_pool(name="x", bufs=N_BLOCKS))
+        stage = ctx.enter_context(tc.tile_pool(name="stage", bufs=2))
+        results = ctx.enter_context(tc.tile_pool(name="results", bufs=4))
+        small = ctx.enter_context(tc.tile_pool(name="small", bufs=3))
+        psum_t = ctx.enter_context(tc.psum_pool(name="psum_t", bufs=4))
+        psum_q = ctx.enter_context(tc.psum_pool(name="psum_q", bufs=4))
+
+        x_of, planes_of, grouped_of, codes_of, scales_of = {}, {}, {}, {}, {}
+        acc_of, q_of, squares_of, sumsq_of = {}, {}, {}, {}
+        norm_of, inverse_of, factor_of = {}, {}, {}
+
+        def load_block(i):
+            b, part = divmod(i, BLOCKS_PER_BATCH)
+            x_sb = x_pool.tile([P, TILES, D_IN], BF16)
+            rows = queries[b, part * BLOCK : (part + 1) * BLOCK, :]
+            nc.sync.dma_start(out=x_sb[:], in_=rows.rearrange("(p t) k -> p t k", t=TILES))
+            x_of[i] = x_sb
+
+        def transpose_block(i):
+            words = x_of[i][:].rearrange("p t k -> p (t k)").bitcast(F32)
+            planes_of[i] = []
+            for pair in range(TILES // 2):
+                planes = psum_t.tile([P, 2, 2, P], F32)
+                for j in range(2):
+                    first = (2 * pair + j) * WORDS
+                    for u in range(2):
+                        nc.tensor.transpose(
+                            planes[:, j, u, :], words[:, first + u : first + WORDS : 2], ident[:]
+                        )
+                planes_of[i].append(planes)
+
+        def regroup_block(i):
+            grouped = stage.tile([P, TILES * D_IN], BF16, align_bytes=64)
+            grouped_words = grouped[:].bitcast(F32)
+            for pair in range(TILES // 2):
+                nc.scalar.copy(
+                    out=grouped_words[:, 2 * pair * WORDS : 2 * (pair + 1) * WORDS].rearrange(
+                        "p (j r u) -> p j r u", j=2, u=2
+                    ),
+                    in_=planes_of[i][pair][:].rearrange("p j u r -> p j r u"),
+                )
+            grouped_of[i] = grouped
+
+        def quantise_block(i):
+            codes = stage.tile([P, TILES * P], U32, align_bytes=64)
+            scales = stage.tile([P, TILES * P], U8, align_bytes=64)
+            nc.vector.quantize_mx(
+                out=codes[:].bitcast(FP8X4), scales=scales[:], in_=grouped_of[i][:]
+            )
+            codes_of[i], scales_of[i] = codes, scales
+
+        def project_block(i):
+            acc_of[i] = []
+            for t in range(TILES):
+                acc = psum_q.tile([P, D_OUT], F32, tag="acc")
+                tokens = slice(t * P, (t + 1) * P)
+                nc.tensor.matmul_mx(
+                    out=acc[:],
+                    lhsT=codes_of[i][:, tokens].bitcast(FP8X4),
+                    lhsT_scale=scales_of[i][:, tokens],
+                    rhs=w_words[:].bitcast(FP4X4),
+                    rhs_scale=w_scales[:],
+                    start=True,
+                    stop=True,
+                )
+                acc_of[i].append(acc)
+
+        def new_results(i):
+            q_of[i] = results.tile([P, HEADS, TILES, D_HEAD], F32, name="q")
+            squares_of[i] = stage.tile([P, TILES, HEADS, D_HEAD], F32, name="squares")
+            sumsq_of[i] = small.tile([P, HEADS, TILES], F32, name="sumsq")
+
+        def bias_and_squares(i, tiles):
+            q, squares, sumsq = q_of[i], squares_of[i], sumsq_of[i]
+            for t in tiles:
+                nc.vector.tensor_tensor(
+                    out=q[:, :, t, :],
+                    in0=acc_of[i][t][:].rearrange("p (h d) -> p h d", h=HEADS),
+                    in1=bias[:].rearrange("p (h d) -> p h d", h=HEADS),
+                    op=ADD,
+                )
+                for h in range(HEADS):
+                    nc.scalar.activation(
+                        out=squares[:, t, h, :],
+                        in_=q[:, h, t, :],
+                        func=SQUARE,
+                        accum_out=sumsq[:, h, t : t + 1],
+                    )
+
+        def norm_block(i):
+            norm = small.tile([P, HEADS, TILES], F32)
+            nc.scalar.sqrt(out=norm[:], in_=sumsq_of[i][:])
+            norm_of[i] = norm
+
+        def invert_norms(i):
+            inverse = small.tile([P, HEADS, TILES], F32)
+            nc.vector.reciprocal(out=inverse[:], in_=norm_of[i][:])
+            inverse_of[i] = inverse
+
+        def apply_gain(i):
+            factor = small.tile([P, HEADS, TILES], F32)
+            nc.vector.tensor_tensor(
+                out=factor[:],
+                in0=inverse_of[i][:],
+                in1=gain[:, 0:HEADS].unsqueeze(2).to_broadcast([P, HEADS, TILES]),
+                op=MULT,
+            )
+            factor_of[i] = factor
+
+        def scale_and_store(i):
+            b, part = divmod(i, BLOCKS_PER_BATCH)
+            q, factor = q_of[i], factor_of[i]
+            n_heads = HEADS // HEAD_SPLIT
+            for g in range(HEAD_SPLIT):
+                heads = slice(g * n_heads, (g + 1) * n_heads)
+                nc.vector.tensor_tensor(
+                    out=q[:, heads, :, :],
+                    in0=q[:, heads, :, :],
+                    in1=factor[:, heads, :].unsqueeze(3).to_broadcast([P, n_heads, TILES, D_HEAD]),
+                    op=MULT,
+                )
+                nc.sync.dma_start(
+                    out=out[b, heads, part * BLOCK : (part + 1) * BLOCK, :].rearrange(
+                        "h (p t) d -> p h (t d)", t=TILES
+                    ),
+                    in_=q[:, heads, :, :].rearrange("p h t d -> p h (t d)"),
+                )
+
+        load_block(0)
+        w_words = consts.tile([P, 2 * D_OUT], U8, align_bytes=64)
+        nc.sync.dma_start(out=w_words[:].bitcast(I32), in_=Wq_words[0].bitcast(I32))
+        w_scales = consts.tile([P, D_OUT], U8, align_bytes=64)
+        nc.vector.memset(w_scales[:].bitcast(I32), 0)
+        for quadrant in range(4):
+            nc.sync.dma_start(
+                out=w_scales[32 * quadrant : 32 * quadrant + 4, :].bitcast(I32),
+                in_=Wq_scales[0, 4 * quadrant : 4 * quadrant + 4, :].bitcast(I32),
+            )
+        for i in range(1, N_BLOCKS):
+            load_block(i)
+
+        ident = consts.tile([P, P], F32)
+        make_identity(nc, ident[:])
+        row0 = consts.tile([P, D_OUT + GAIN_PAD], BF16)
+        nc.vector.memset(row0[:], 0.0)
+        nc.scalar.dma_start(out=row0[0:1, 0:D_OUT], in_=bq.rearrange("(o n) -> o n", o=1))
+        nc.scalar.dma_start(
+            out=row0[0:1, D_OUT : D_OUT + HEADS], in_=gamma.rearrange("a h b c -> a (h b c)")
+        )
+        ones = consts.tile([P, P], BF16)
+        nc.vector.memset(ones[:], 1.0)
+        one = consts.tile([P, 1], F32)
+        nc.vector.memset(one[:], 1.0)
+        warm = consts.tile([P, 1], F32)
+        nc.scalar.sqrt(out=warm[:], in_=one[:])
+
+        transpose_block(0)
+
+        bias = consts.tile([P, D_OUT], F32)
+        gain = consts.tile([P, GAIN_PAD], F32)
+        bias_ps = psum_q.tile([P, D_OUT], F32, tag="acc")
+        nc.tensor.matmul(out=bias_ps[:], lhsT=ones[:], rhs=row0[:, 0:D_OUT], start=True, stop=True)
+        nc.vector.tensor_copy(out=bias[:], in_=bias_ps[:])
+        gain_ps = psum_q.tile([P, D_OUT], F32, tag="acc")
+        nc.tensor.matmul(
+            out=gain_ps[:, 0:GAIN_PAD], lhsT=ones[:], rhs=row0[:, D_OUT:], start=True, stop=True
+        )
+        nc.vector.tensor_copy(out=gain[:], in_=gain_ps[:, 0:GAIN_PAD])
+
+        regroup_block(0)
+        quantise_block(0)
+        project_block(0)
+        transpose_block(1)
+
+        for i in range(N_BLOCKS):
+            if i + 1 < N_BLOCKS:
+                regroup_block(i + 1)
+            new_results(i)
+            if i >= 1:
+                invert_norms(i - 1)
+            bias_and_squares(i, range(0, TILES // 2))
+            if i >= 1:
+                apply_gain(i - 1)
+            bias_and_squares(i, range(TILES // 2, TILES))
+            if i + 1 < N_BLOCKS:
+                quantise_block(i + 1)
+                project_block(i + 1)
+            if i + 2 < N_BLOCKS:
+                transpose_block(i + 2)
+            norm_block(i)
+            if i >= 1:
+                scale_and_store(i - 1)
+        invert_norms(N_BLOCKS - 1)
+        apply_gain(N_BLOCKS - 1)
+        scale_and_store(N_BLOCKS - 1)

@@ -13,17 +13,17 @@ FP4X4 = mybir.dt.float4_e2m1fn_x4
 ADD = mybir.AluOpType.add
 MULT = mybir.AluOpType.mult
 SQUARE = mybir.ActivationFunctionType.Square
+RSQRT = mybir.ActivationFunctionType.Abs_reciprocal_sqrt
 
 P = 128
 BATCH, TOKENS, D_IN = 4, 1024, 512
 HEADS, D_HEAD = 8, 64
 D_OUT = HEADS * D_HEAD
-TILES = 4
+TILES = 2
 BLOCK = P * TILES
 BLOCKS_PER_BATCH = TOKENS // BLOCK
 N_BLOCKS = BATCH * BLOCKS_PER_BATCH
 WORDS = D_IN // 2
-HEAD_SPLIT = 2
 GAIN_PAD = 32
 
 FLOPS = 2 * BATCH * TOKENS * D_IN * D_OUT
@@ -36,14 +36,14 @@ def tile_ufoattention_pb_kernel(tc, queries, Wq_words, Wq_scales, bq, gamma, out
         consts = ctx.enter_context(tc.tile_pool(name="consts", bufs=1))
         x_pool = ctx.enter_context(tc.tile_pool(name="x", bufs=N_BLOCKS))
         stage = ctx.enter_context(tc.tile_pool(name="stage", bufs=2))
-        results = ctx.enter_context(tc.tile_pool(name="results", bufs=4))
+        results = ctx.enter_context(tc.tile_pool(name="results", bufs=8))
         small = ctx.enter_context(tc.tile_pool(name="small", bufs=3))
         psum_t = ctx.enter_context(tc.psum_pool(name="psum_t", bufs=4))
         psum_q = ctx.enter_context(tc.psum_pool(name="psum_q", bufs=4))
 
         x_of, planes_of, grouped_of, codes_of, scales_of = {}, {}, {}, {}, {}
         acc_of, q_of, squares_of, sumsq_of = {}, {}, {}, {}
-        norm_of, inverse_of, factor_of = {}, {}, {}
+        inverse_of, factor_of = {}, {}
 
         def load_block(i):
             b, part = divmod(i, BLOCKS_PER_BATCH)
@@ -68,8 +68,9 @@ def tile_ufoattention_pb_kernel(tc, queries, Wq_words, Wq_scales, bq, gamma, out
         def regroup_block(i):
             grouped = stage.tile([P, TILES * D_IN], BF16, align_bytes=64)
             grouped_words = grouped[:].bitcast(F32)
+            copy = nc.scalar.copy if i % 2 == 0 else nc.vector.tensor_copy
             for pair in range(TILES // 2):
-                nc.scalar.copy(
+                copy(
                     out=grouped_words[:, 2 * pair * WORDS : 2 * (pair + 1) * WORDS].rearrange(
                         "p (j r u) -> p j r u", j=2, u=2
                     ),
@@ -123,14 +124,9 @@ def tile_ufoattention_pb_kernel(tc, queries, Wq_words, Wq_scales, bq, gamma, out
                         accum_out=sumsq[:, h, t : t + 1],
                     )
 
-        def norm_block(i):
-            norm = small.tile([P, HEADS, TILES], F32)
-            nc.scalar.sqrt(out=norm[:], in_=sumsq_of[i][:])
-            norm_of[i] = norm
-
         def invert_norms(i):
             inverse = small.tile([P, HEADS, TILES], F32)
-            nc.vector.reciprocal(out=inverse[:], in_=norm_of[i][:])
+            nc.scalar.activation(out=inverse[:], in_=sumsq_of[i][:], func=RSQRT)
             inverse_of[i] = inverse
 
         def apply_gain(i):
@@ -146,10 +142,10 @@ def tile_ufoattention_pb_kernel(tc, queries, Wq_words, Wq_scales, bq, gamma, out
         def scale_and_store(i):
             b, part = divmod(i, BLOCKS_PER_BATCH)
             q, factor = q_of[i], factor_of[i]
-            n_heads = HEADS // HEAD_SPLIT
-            for g in range(HEAD_SPLIT):
+            n_heads = HEADS // 2
+            for g, engine in enumerate((nc.vector, nc.gpsimd)):
                 heads = slice(g * n_heads, (g + 1) * n_heads)
-                nc.vector.tensor_tensor(
+                engine.tensor_tensor(
                     out=q[:, heads, :, :],
                     in0=q[:, heads, :, :],
                     in1=factor[:, heads, :].unsqueeze(3).to_broadcast([P, n_heads, TILES, D_HEAD]),
@@ -188,7 +184,7 @@ def tile_ufoattention_pb_kernel(tc, queries, Wq_words, Wq_scales, bq, gamma, out
         one = consts.tile([P, 1], F32)
         nc.vector.memset(one[:], 1.0)
         warm = consts.tile([P, 1], F32)
-        nc.scalar.sqrt(out=warm[:], in_=one[:])
+        nc.scalar.activation(out=warm[:], in_=one[:], func=RSQRT)
 
         transpose_block(0)
 
@@ -209,23 +205,19 @@ def tile_ufoattention_pb_kernel(tc, queries, Wq_words, Wq_scales, bq, gamma, out
         transpose_block(1)
 
         for i in range(N_BLOCKS):
+            if i + 2 < N_BLOCKS:
+                transpose_block(i + 2)
             if i + 1 < N_BLOCKS:
                 regroup_block(i + 1)
             new_results(i)
-            if i >= 1:
-                invert_norms(i - 1)
-            bias_and_squares(i, range(0, TILES // 2))
+            bias_and_squares(i, range(TILES))
+            invert_norms(i)
             if i >= 1:
                 apply_gain(i - 1)
-            bias_and_squares(i, range(TILES // 2, TILES))
             if i + 1 < N_BLOCKS:
                 quantise_block(i + 1)
                 project_block(i + 1)
-            if i + 2 < N_BLOCKS:
-                transpose_block(i + 2)
-            norm_block(i)
             if i >= 1:
                 scale_and_store(i - 1)
-        invert_norms(N_BLOCKS - 1)
         apply_gain(N_BLOCKS - 1)
         scale_and_store(N_BLOCKS - 1)

@@ -24,6 +24,7 @@ BLOCK = P * TILES
 BLOCKS_PER_BATCH = TOKENS // BLOCK
 N_BLOCKS = BATCH * BLOCKS_PER_BATCH
 WORDS = D_IN // 2
+HEAD_SPLIT = 1
 GAIN_PAD = 32
 
 FLOPS = 2 * BATCH * TOKENS * D_IN * D_OUT
@@ -36,7 +37,7 @@ def tile_ufoattention_pb_kernel(tc, queries, Wq_words, Wq_scales, bq, gamma, out
         consts = ctx.enter_context(tc.tile_pool(name="consts", bufs=1))
         x_pool = ctx.enter_context(tc.tile_pool(name="x", bufs=N_BLOCKS))
         stage = ctx.enter_context(tc.tile_pool(name="stage", bufs=2))
-        results = ctx.enter_context(tc.tile_pool(name="results", bufs=8))
+        results = ctx.enter_context(tc.tile_pool(name="results", bufs=4))
         small = ctx.enter_context(tc.tile_pool(name="small", bufs=3))
         psum_t = ctx.enter_context(tc.psum_pool(name="psum_t", bufs=4))
         psum_q = ctx.enter_context(tc.psum_pool(name="psum_q", bufs=4))
@@ -68,9 +69,8 @@ def tile_ufoattention_pb_kernel(tc, queries, Wq_words, Wq_scales, bq, gamma, out
         def regroup_block(i):
             grouped = stage.tile([P, TILES * D_IN], BF16, align_bytes=64)
             grouped_words = grouped[:].bitcast(F32)
-            copy = nc.scalar.copy if i % 2 == 0 else nc.vector.tensor_copy
             for pair in range(TILES // 2):
-                copy(
+                nc.scalar.copy(
                     out=grouped_words[:, 2 * pair * WORDS : 2 * (pair + 1) * WORDS].rearrange(
                         "p (j r u) -> p j r u", j=2, u=2
                     ),
@@ -142,10 +142,10 @@ def tile_ufoattention_pb_kernel(tc, queries, Wq_words, Wq_scales, bq, gamma, out
         def scale_and_store(i):
             b, part = divmod(i, BLOCKS_PER_BATCH)
             q, factor = q_of[i], factor_of[i]
-            n_heads = HEADS // 2
-            for g, engine in enumerate((nc.vector, nc.gpsimd)):
+            n_heads = HEADS // HEAD_SPLIT
+            for g in range(HEAD_SPLIT):
                 heads = slice(g * n_heads, (g + 1) * n_heads)
-                engine.tensor_tensor(
+                nc.vector.tensor_tensor(
                     out=q[:, heads, :, :],
                     in0=q[:, heads, :, :],
                     in1=factor[:, heads, :].unsqueeze(3).to_broadcast([P, n_heads, TILES, D_HEAD]),

@@ -24,7 +24,7 @@ BLOCK = P * TILES
 BLOCKS_PER_BATCH = TOKENS // BLOCK
 N_BLOCKS = BATCH * BLOCKS_PER_BATCH
 WORDS = D_IN // 2
-HEAD_SPLIT = 1
+VECTOR_HEADS = 3
 GAIN_PAD = 32
 
 FLOPS = 2 * BATCH * TOKENS * D_IN * D_OUT
@@ -37,7 +37,7 @@ def tile_ufoattention_pb_kernel(tc, queries, Wq_words, Wq_scales, bq, gamma, out
         consts = ctx.enter_context(tc.tile_pool(name="consts", bufs=1))
         x_pool = ctx.enter_context(tc.tile_pool(name="x", bufs=N_BLOCKS))
         stage = ctx.enter_context(tc.tile_pool(name="stage", bufs=2))
-        results = ctx.enter_context(tc.tile_pool(name="results", bufs=4))
+        results = ctx.enter_context(tc.tile_pool(name="results", bufs=8))
         small = ctx.enter_context(tc.tile_pool(name="small", bufs=3))
         psum_t = ctx.enter_context(tc.psum_pool(name="psum_t", bufs=4))
         psum_q = ctx.enter_context(tc.psum_pool(name="psum_q", bufs=4))
@@ -66,11 +66,11 @@ def tile_ufoattention_pb_kernel(tc, queries, Wq_words, Wq_scales, bq, gamma, out
                         )
                 planes_of[i].append(planes)
 
-        def regroup_block(i):
+        def regroup_block(i, copy):
             grouped = stage.tile([P, TILES * D_IN], BF16, align_bytes=64)
             grouped_words = grouped[:].bitcast(F32)
             for pair in range(TILES // 2):
-                nc.scalar.copy(
+                copy(
                     out=grouped_words[:, 2 * pair * WORDS : 2 * (pair + 1) * WORDS].rearrange(
                         "p (j r u) -> p j r u", j=2, u=2
                     ),
@@ -142,21 +142,20 @@ def tile_ufoattention_pb_kernel(tc, queries, Wq_words, Wq_scales, bq, gamma, out
         def scale_and_store(i):
             b, part = divmod(i, BLOCKS_PER_BATCH)
             q, factor = q_of[i], factor_of[i]
-            n_heads = HEADS // HEAD_SPLIT
-            for g in range(HEAD_SPLIT):
-                heads = slice(g * n_heads, (g + 1) * n_heads)
-                nc.vector.tensor_tensor(
+            for engine, first, last in ((nc.vector, 0, VECTOR_HEADS), (nc.gpsimd, VECTOR_HEADS, HEADS)):
+                heads, n_heads = slice(first, last), last - first
+                engine.tensor_tensor(
                     out=q[:, heads, :, :],
                     in0=q[:, heads, :, :],
                     in1=factor[:, heads, :].unsqueeze(3).to_broadcast([P, n_heads, TILES, D_HEAD]),
                     op=MULT,
                 )
-                nc.sync.dma_start(
-                    out=out[b, heads, part * BLOCK : (part + 1) * BLOCK, :].rearrange(
-                        "h (p t) d -> p h (t d)", t=TILES
-                    ),
-                    in_=q[:, heads, :, :].rearrange("p h t d -> p h (t d)"),
-                )
+            nc.sync.dma_start(
+                out=out[b, :, part * BLOCK : (part + 1) * BLOCK, :].rearrange(
+                    "h (p t) d -> p h (t d)", t=TILES
+                ),
+                in_=q[:].rearrange("p h t d -> p h (t d)"),
+            )
 
         load_block(0)
         w_words = consts.tile([P, 2 * D_OUT], U8, align_bytes=64)
@@ -187,36 +186,38 @@ def tile_ufoattention_pb_kernel(tc, queries, Wq_words, Wq_scales, bq, gamma, out
         nc.scalar.activation(out=warm[:], in_=one[:], func=RSQRT)
 
         transpose_block(0)
+        regroup_block(0, nc.scalar.copy)
 
         bias = consts.tile([P, D_OUT], F32)
         gain = consts.tile([P, GAIN_PAD], F32)
         bias_ps = psum_q.tile([P, D_OUT], F32, tag="acc")
         nc.tensor.matmul(out=bias_ps[:], lhsT=ones[:], rhs=row0[:, 0:D_OUT], start=True, stop=True)
-        nc.vector.tensor_copy(out=bias[:], in_=bias_ps[:])
+        nc.scalar.copy(out=bias[:], in_=bias_ps[:])
         gain_ps = psum_q.tile([P, D_OUT], F32, tag="acc")
         nc.tensor.matmul(
             out=gain_ps[:, 0:GAIN_PAD], lhsT=ones[:], rhs=row0[:, D_OUT:], start=True, stop=True
         )
-        nc.vector.tensor_copy(out=gain[:], in_=gain_ps[:, 0:GAIN_PAD])
+        nc.scalar.copy(out=gain[:], in_=gain_ps[:, 0:GAIN_PAD])
 
-        regroup_block(0)
+        transpose_block(1)
+        regroup_block(1, nc.scalar.copy)
         quantise_block(0)
         project_block(0)
-        transpose_block(1)
 
         for i in range(N_BLOCKS):
             if i + 2 < N_BLOCKS:
                 transpose_block(i + 2)
-            if i + 1 < N_BLOCKS:
-                regroup_block(i + 1)
             new_results(i)
-            bias_and_squares(i, range(TILES))
-            invert_norms(i)
-            if i >= 1:
-                apply_gain(i - 1)
+            bias_and_squares(i, range(0, TILES // 2))
             if i + 1 < N_BLOCKS:
                 quantise_block(i + 1)
                 project_block(i + 1)
+            bias_and_squares(i, range(TILES // 2, TILES))
+            invert_norms(i)
+            if i >= 1:
+                apply_gain(i - 1)
+            if i + 2 < N_BLOCKS:
+                regroup_block(i + 2, nc.vector.tensor_copy)
             if i >= 1:
                 scale_and_store(i - 1)
         apply_gain(N_BLOCKS - 1)

@@ -202,22 +202,22 @@ def tile_ufoattention_pb_kernel(tc, queries, Wq_words, Wq_scales, bq, gamma, out
         transpose_block(1)
         regroup_block(1, nc.scalar.copy)
         quantise_block(0)
+        transpose_block(2)
         project_block(0)
 
         for i in range(N_BLOCKS):
+            if i + 3 < N_BLOCKS:
+                transpose_block(i + 3)
             if i + 2 < N_BLOCKS:
-                transpose_block(i + 2)
+                regroup_block(i + 2, nc.vector.tensor_copy)
             new_results(i)
-            bias_and_squares(i, range(0, TILES // 2))
-            if i + 1 < N_BLOCKS:
-                quantise_block(i + 1)
-                project_block(i + 1)
-            bias_and_squares(i, range(TILES // 2, TILES))
+            bias_and_squares(i, range(TILES))
             invert_norms(i)
             if i >= 1:
                 apply_gain(i - 1)
-            if i + 2 < N_BLOCKS:
-                regroup_block(i + 2, nc.vector.tensor_copy)
+            if i + 1 < N_BLOCKS:
+                quantise_block(i + 1)
+                project_block(i + 1)
             if i >= 1:
                 scale_and_store(i - 1)
         apply_gain(N_BLOCKS - 1)

@@ -204,20 +204,24 @@ def tile_ufoattention_pb_kernel(tc, queries, Wq_words, Wq_scales, bq, gamma, out
         quantise_block(0)
         transpose_block(2)
         project_block(0)
+        regroup_block(2, nc.scalar.copy)
+        quantise_block(1)
+        transpose_block(3)
 
         for i in range(N_BLOCKS):
-            if i + 3 < N_BLOCKS:
-                transpose_block(i + 3)
-            if i + 2 < N_BLOCKS:
-                regroup_block(i + 2, nc.vector.tensor_copy)
+            if i + 1 < N_BLOCKS:
+                project_block(i + 1)
+            if i + 4 < N_BLOCKS:
+                transpose_block(i + 4)
             new_results(i)
             bias_and_squares(i, range(TILES))
+            if i + 3 < N_BLOCKS:
+                regroup_block(i + 3, nc.vector.tensor_copy)
             invert_norms(i)
             if i >= 1:
                 apply_gain(i - 1)
-            if i + 1 < N_BLOCKS:
-                quantise_block(i + 1)
-                project_block(i + 1)
+            if i + 2 < N_BLOCKS:
+                quantise_block(i + 2)
             if i >= 1:
                 scale_and_store(i - 1)
         apply_gain(N_BLOCKS - 1)

@@ -14,17 +14,19 @@ ADD = mybir.AluOpType.add
 MULT = mybir.AluOpType.mult
 SQUARE = mybir.ActivationFunctionType.Square
 RSQRT = mybir.ActivationFunctionType.Abs_reciprocal_sqrt
+COPY = mybir.ActivationFunctionType.Copy
 
 P = 128
 BATCH, TOKENS, D_IN = 4, 1024, 512
 HEADS, D_HEAD = 8, 64
 D_OUT = HEADS * D_HEAD
-TILES = 2
-BLOCK = P * TILES
-BLOCKS_PER_BATCH = TOKENS // BLOCK
-N_BLOCKS = BATCH * BLOCKS_PER_BATCH
 WORDS = D_IN // 2
-VECTOR_HEADS = 3
+SIZES = ((2, 2, 2, 2), (2, 2, 2, 2), (2, 2, 2, 2), (2, 2, 2, 2))
+MAX_TILES = 2
+ACC_BANKS = 4
+SPLIT = (2, 1)
+SPLIT_BEFORE_LAST = (2, 1)
+SPLIT_LAST = (2, 1)
 GAIN_PAD = 32
 
 FLOPS = 2 * BATCH * TOKENS * D_IN * D_OUT
@@ -32,34 +34,46 @@ FLOPS = 2 * BATCH * TOKENS * D_IN * D_OUT
 
 def tile_ufoattention_pb_kernel(tc, queries, Wq_words, Wq_scales, bq, gamma, out):
     nc = tc.nc
+    blocks = []
+    for b in range(BATCH):
+        first_token = 0
+        for tiles in SIZES[b]:
+            blocks.append((b, first_token, tiles))
+            first_token += tiles * P
+        assert first_token == TOKENS
+    n_blocks = len(blocks)
+
     with ExitStack() as ctx:
         ctx.enter_context(tc.manual_schedule())
         consts = ctx.enter_context(tc.tile_pool(name="consts", bufs=1))
-        x_pool = ctx.enter_context(tc.tile_pool(name="x", bufs=N_BLOCKS))
+        x_pool = ctx.enter_context(tc.tile_pool(name="x", bufs=n_blocks))
         stage = ctx.enter_context(tc.tile_pool(name="stage", bufs=2))
         results = ctx.enter_context(tc.tile_pool(name="results", bufs=8))
         small = ctx.enter_context(tc.tile_pool(name="small", bufs=3))
-        psum_t = ctx.enter_context(tc.psum_pool(name="psum_t", bufs=4))
-        psum_q = ctx.enter_context(tc.psum_pool(name="psum_q", bufs=4))
+        psum_t = ctx.enter_context(tc.psum_pool(name="psum_t", bufs=8 - ACC_BANKS))
+        psum_q = ctx.enter_context(tc.psum_pool(name="psum_q", bufs=ACC_BANKS))
 
         x_of, planes_of, grouped_of, codes_of, scales_of = {}, {}, {}, {}, {}
         acc_of, q_of, squares_of, sumsq_of = {}, {}, {}, {}
         inverse_of, factor_of = {}, {}
 
         def load_block(i):
-            b, part = divmod(i, BLOCKS_PER_BATCH)
-            x_sb = x_pool.tile([P, TILES, D_IN], BF16)
-            rows = queries[b, part * BLOCK : (part + 1) * BLOCK, :]
-            nc.sync.dma_start(out=x_sb[:], in_=rows.rearrange("(p t) k -> p t k", t=TILES))
+            b, first, tiles = blocks[i]
+            x_sb = x_pool.tile([P, MAX_TILES, D_IN], BF16)
+            rows = queries[b, first : first + tiles * P, :]
+            nc.sync.dma_start(
+                out=x_sb[:, 0:tiles, :], in_=rows.rearrange("(p t) k -> p t k", t=tiles)
+            )
             x_of[i] = x_sb
 
         def transpose_block(i):
+            tiles = blocks[i][2]
             words = x_of[i][:].rearrange("p t k -> p (t k)").bitcast(F32)
             planes_of[i] = []
-            for pair in range(TILES // 2):
+            for t0 in range(0, tiles, 2):
                 planes = psum_t.tile([P, 2, 2, P], F32)
-                for j in range(2):
-                    first = (2 * pair + j) * WORDS
+                for j in range(min(2, tiles - t0)):
+                    first = (t0 + j) * WORDS
                     for u in range(2):
                         nc.tensor.transpose(
                             planes[:, j, u, :], words[:, first + u : first + WORDS : 2], ident[:]
@@ -67,28 +81,33 @@ def tile_ufoattention_pb_kernel(tc, queries, Wq_words, Wq_scales, bq, gamma, out
                 planes_of[i].append(planes)
 
         def regroup_block(i, copy):
-            grouped = stage.tile([P, TILES * D_IN], BF16, align_bytes=64)
+            tiles = blocks[i][2]
+            grouped = stage.tile([P, MAX_TILES * D_IN], BF16, align_bytes=64)
             grouped_words = grouped[:].bitcast(F32)
-            for pair in range(TILES // 2):
+            for t0 in range(0, tiles, 2):
+                n = min(2, tiles - t0)
                 copy(
-                    out=grouped_words[:, 2 * pair * WORDS : 2 * (pair + 1) * WORDS].rearrange(
-                        "p (j r u) -> p j r u", j=2, u=2
+                    out=grouped_words[:, t0 * WORDS : (t0 + n) * WORDS].rearrange(
+                        "p (j r u) -> p j r u", j=n, u=2
                     ),
-                    in_=planes_of[i][pair][:].rearrange("p j u r -> p j r u"),
+                    in_=planes_of[i][t0 // 2][:, 0:n, :, :].rearrange("p j u r -> p j r u"),
                 )
             grouped_of[i] = grouped
 
         def quantise_block(i):
-            codes = stage.tile([P, TILES * P], U32, align_bytes=64)
-            scales = stage.tile([P, TILES * P], U8, align_bytes=64)
+            tiles = blocks[i][2]
+            codes = stage.tile([P, MAX_TILES * P], U32, align_bytes=64)
+            scales = stage.tile([P, MAX_TILES * P], U8, align_bytes=64)
             nc.vector.quantize_mx(
-                out=codes[:].bitcast(FP8X4), scales=scales[:], in_=grouped_of[i][:]
+                out=codes[:, 0 : tiles * P].bitcast(FP8X4),
+                scales=scales[:, 0 : tiles * P],
+                in_=grouped_of[i][:, 0 : tiles * D_IN],
             )
             codes_of[i], scales_of[i] = codes, scales
-
-        def project_block(i):
             acc_of[i] = []
-            for t in range(TILES):
+
+        def project_tiles(i, count):
+            for t in range(len(acc_of[i]), min(len(acc_of[i]) + count, blocks[i][2])):
                 acc = psum_q.tile([P, D_OUT], F32, tag="acc")
                 tokens = slice(t * P, (t + 1) * P)
                 nc.tensor.matmul_mx(
@@ -103,58 +122,76 @@ def tile_ufoattention_pb_kernel(tc, queries, Wq_words, Wq_scales, bq, gamma, out
                 acc_of[i].append(acc)
 
         def new_results(i):
-            q_of[i] = results.tile([P, HEADS, TILES, D_HEAD], F32, name="q")
-            squares_of[i] = stage.tile([P, TILES, HEADS, D_HEAD], F32, name="squares")
-            sumsq_of[i] = small.tile([P, HEADS, TILES], F32, name="sumsq")
+            q_of[i] = results.tile([P, HEADS, MAX_TILES, D_HEAD], F32, name="q")
+            squares_of[i] = stage.tile([P, MAX_TILES, HEADS, D_HEAD], F32, name="squares")
+            sumsq_of[i] = small.tile([P, HEADS, MAX_TILES], F32, name="sumsq")
 
-        def bias_and_squares(i, tiles):
+        def bias_and_squares(i, t):
             q, squares, sumsq = q_of[i], squares_of[i], sumsq_of[i]
-            for t in tiles:
-                nc.vector.tensor_tensor(
-                    out=q[:, :, t, :],
-                    in0=acc_of[i][t][:].rearrange("p (h d) -> p h d", h=HEADS),
-                    in1=bias[:].rearrange("p (h d) -> p h d", h=HEADS),
-                    op=ADD,
+            nc.vector.tensor_tensor(
+                out=q[:, :, t, :],
+                in0=acc_of[i][t][:].rearrange("p (h d) -> p h d", h=HEADS),
+                in1=bias[:].rearrange("p (h d) -> p h d", h=HEADS),
+                op=ADD,
+            )
+            for h in range(HEADS):
+                nc.scalar.activation(
+                    out=squares[:, t, h, :],
+                    in_=q[:, h, t, :],
+                    func=SQUARE,
+                    accum_out=sumsq[:, h, t : t + 1],
                 )
-                for h in range(HEADS):
-                    nc.scalar.activation(
-                        out=squares[:, t, h, :],
-                        in_=q[:, h, t, :],
-                        func=SQUARE,
-                        accum_out=sumsq[:, h, t : t + 1],
-                    )
 
         def invert_norms(i):
-            inverse = small.tile([P, HEADS, TILES], F32)
-            nc.scalar.activation(out=inverse[:], in_=sumsq_of[i][:], func=RSQRT)
+            tiles = blocks[i][2]
+            inverse = small.tile([P, HEADS, MAX_TILES], F32)
+            nc.scalar.activation(
+                out=inverse[:, :, 0:tiles], in_=sumsq_of[i][:, :, 0:tiles], func=RSQRT
+            )
             inverse_of[i] = inverse
 
         def apply_gain(i):
-            factor = small.tile([P, HEADS, TILES], F32)
+            tiles = blocks[i][2]
+            factor = small.tile([P, HEADS, MAX_TILES], F32)
             nc.vector.tensor_tensor(
-                out=factor[:],
-                in0=inverse_of[i][:],
-                in1=gain[:, 0:HEADS].unsqueeze(2).to_broadcast([P, HEADS, TILES]),
+                out=factor[:, :, 0:tiles],
+                in0=inverse_of[i][:, :, 0:tiles],
+                in1=gain[:, 0:HEADS].unsqueeze(2).to_broadcast([P, HEADS, tiles]),
                 op=MULT,
             )
             factor_of[i] = factor
 
         def scale_and_store(i):
-            b, part = divmod(i, BLOCKS_PER_BATCH)
+            b, first, tiles = blocks[i]
             q, factor = q_of[i], factor_of[i]
-            for engine, first, last in ((nc.vector, 0, VECTOR_HEADS), (nc.gpsimd, VECTOR_HEADS, HEADS)):
-                heads, n_heads = slice(first, last), last - first
-                engine.tensor_tensor(
-                    out=q[:, heads, :, :],
-                    in0=q[:, heads, :, :],
-                    in1=factor[:, heads, :].unsqueeze(3).to_broadcast([P, n_heads, TILES, D_HEAD]),
-                    op=MULT,
-                )
+            by_vector, by_scalar = SPLIT
+            if i == n_blocks - 2:
+                by_vector, by_scalar = SPLIT_BEFORE_LAST
+            if i == n_blocks - 1:
+                by_vector, by_scalar = SPLIT_LAST
+            for engine, h0, h1 in (
+                (nc.vector, 0, by_vector),
+                (nc.gpsimd, by_vector + by_scalar, HEADS),
+            ):
+                if h1 > h0:
+                    engine.tensor_tensor(
+                        out=q[:, h0:h1, 0:tiles, :],
+                        in0=q[:, h0:h1, 0:tiles, :],
+                        in1=factor[:, h0:h1, 0:tiles]
+                        .unsqueeze(3)
+                        .to_broadcast([P, h1 - h0, tiles, D_HEAD]),
+                        op=MULT,
+                    )
+            for h in range(by_vector, by_vector + by_scalar):
+                for t in range(tiles):
+                    nc.scalar.activation(
+                        out=q[:, h, t, :], in_=q[:, h, t, :], func=COPY, scale=factor[:, h, t : t + 1]
+                    )
             nc.sync.dma_start(
-                out=out[b, :, part * BLOCK : (part + 1) * BLOCK, :].rearrange(
-                    "h (p t) d -> p h (t d)", t=TILES
+                out=out[b, :, first : first + tiles * P, :].rearrange(
+                    "h (p t) d -> p h (t d)", t=tiles
                 ),
-                in_=q[:].rearrange("p h t d -> p h (t d)"),
+                in_=q[:, :, 0:tiles, :].rearrange("p h t d -> p h (t d)"),
             )
 
         load_block(0)
@@ -167,7 +204,7 @@ def tile_ufoattention_pb_kernel(tc, queries, Wq_words, Wq_scales, bq, gamma, out
                 out=w_scales[32 * quadrant : 32 * quadrant + 4, :].bitcast(I32),
                 in_=Wq_scales[0, 4 * quadrant : 4 * quadrant + 4, :].bitcast(I32),
             )
-        for i in range(1, N_BLOCKS):
+        for i in range(1, n_blocks):
             load_block(i)
 
         ident = consts.tile([P, P], F32)
@@ -203,26 +240,30 @@ def tile_ufoattention_pb_kernel(tc, queries, Wq_words, Wq_scales, bq, gamma, out
         regroup_block(1, nc.scalar.copy)
         quantise_block(0)
         transpose_block(2)
-        project_block(0)
+        project_tiles(0, ACC_BANKS)
         regroup_block(2, nc.scalar.copy)
         quantise_block(1)
         transpose_block(3)
 
-        for i in range(N_BLOCKS):
-            if i + 1 < N_BLOCKS:
-                project_block(i + 1)
-            if i + 4 < N_BLOCKS:
+        for i in range(n_blocks):
+            tiles = blocks[i][2]
+            if i + 1 < n_blocks:
+                project_tiles(i + 1, ACC_BANKS - tiles)
+            if i + 4 < n_blocks:
                 transpose_block(i + 4)
             new_results(i)
-            bias_and_squares(i, range(TILES))
-            if i + 3 < N_BLOCKS:
+            for t in range(tiles):
+                bias_and_squares(i, t)
+                if i + 1 < n_blocks:
+                    project_tiles(i + 1, 1)
+            if i + 3 < n_blocks:
                 regroup_block(i + 3, nc.vector.tensor_copy)
             invert_norms(i)
             if i >= 1:
                 apply_gain(i - 1)
-            if i + 2 < N_BLOCKS:
+            if i + 2 < n_blocks:
                 quantise_block(i + 2)
             if i >= 1:
                 scale_and_store(i - 1)
-        apply_gain(N_BLOCKS - 1)
-        scale_and_store(N_BLOCKS - 1)
+        apply_gain(n_blocks - 1)
+        scale_and_store(n_blocks - 1)

@@ -27,6 +27,8 @@ ACC_BANKS = 4
 SPLIT = (2, 1)
 SPLIT_BEFORE_LAST = (2, 1)
 SPLIT_LAST = (2, 1)
+PASSES = 2
+FIRST_REPEATED = 3
 GAIN_PAD = 32
 
 FLOPS = 2 * BATCH * TOKENS * D_IN * D_OUT
@@ -110,15 +112,16 @@ def tile_ufoattention_pb_kernel(tc, queries, Wq_words, Wq_scales, bq, gamma, out
             for t in range(len(acc_of[i]), min(len(acc_of[i]) + count, blocks[i][2])):
                 acc = psum_q.tile([P, D_OUT], F32, tag="acc")
                 tokens = slice(t * P, (t + 1) * P)
-                nc.tensor.matmul_mx(
-                    out=acc[:],
-                    lhsT=codes_of[i][:, tokens].bitcast(FP8X4),
-                    lhsT_scale=scales_of[i][:, tokens],
-                    rhs=w_words[:].bitcast(FP4X4),
-                    rhs_scale=w_scales[:],
-                    start=True,
-                    stop=True,
-                )
+                for rep in range(PASSES if i >= FIRST_REPEATED else 1):
+                    nc.tensor.matmul_mx(
+                        out=acc[:],
+                        lhsT=codes_of[i][:, tokens].bitcast(FP8X4),
+                        lhsT_scale=scales_of[i][:, tokens],
+                        rhs=w_words[:].bitcast(FP4X4),
+                        rhs_scale=w_scales[:],
+                        start=True,
+                        stop=True,
+                    )
                 acc_of[i].append(acc)
 
         def new_results(i):

@@ -24,9 +24,10 @@ WORDS = D_IN // 2
 SIZES = ((2, 2, 2, 2), (2, 2, 2, 2), (2, 2, 2, 2), (2, 2, 2, 2))
 MAX_TILES = 2
 ACC_BANKS = 4
-SPLIT = (2, 1)
-SPLIT_BEFORE_LAST = (2, 1)
-SPLIT_LAST = (2, 1)
+SPLIT = (0, 3)
+SPLIT_BEFORE_LAST = (5, 3)
+SPLIT_LAST = (5, 3)
+STATS_HEADS = 4
 PASSES = 2
 FIRST_REPEATED = 3
 GAIN_PAD = 32
@@ -49,15 +50,15 @@ def tile_ufoattention_pb_kernel(tc, queries, Wq_words, Wq_scales, bq, gamma, out
         ctx.enter_context(tc.manual_schedule())
         consts = ctx.enter_context(tc.tile_pool(name="consts", bufs=1))
         x_pool = ctx.enter_context(tc.tile_pool(name="x", bufs=n_blocks))
-        stage = ctx.enter_context(tc.tile_pool(name="stage", bufs=2))
+        stage = ctx.enter_context(tc.tile_pool(name="stage", bufs=4))
         results = ctx.enter_context(tc.tile_pool(name="results", bufs=8))
-        small = ctx.enter_context(tc.tile_pool(name="small", bufs=3))
+        small = ctx.enter_context(tc.tile_pool(name="small", bufs=6))
         psum_t = ctx.enter_context(tc.psum_pool(name="psum_t", bufs=8 - ACC_BANKS))
         psum_q = ctx.enter_context(tc.psum_pool(name="psum_q", bufs=ACC_BANKS))
 
         x_of, planes_of, grouped_of, codes_of, scales_of = {}, {}, {}, {}, {}
         acc_of, q_of, squares_of, sumsq_of = {}, {}, {}, {}
-        inverse_of, factor_of = {}, {}
+        inverse_of, factor_of, stats_of, msq_of = {}, {}, {}, {}
 
         def load_block(i):
             b, first, tiles = blocks[i]
@@ -127,39 +128,63 @@ def tile_ufoattention_pb_kernel(tc, queries, Wq_words, Wq_scales, bq, gamma, out
         def new_results(i):
             q_of[i] = results.tile([P, HEADS, MAX_TILES, D_HEAD], F32, name="q")
             squares_of[i] = stage.tile([P, MAX_TILES, HEADS, D_HEAD], F32, name="squares")
-            sumsq_of[i] = small.tile([P, HEADS, MAX_TILES], F32, name="sumsq")
+            sumsq_of[i] = small.tile([P, MAX_TILES, HEADS], F32, name="sumsq")
+            stats_of[i] = small.tile([P, MAX_TILES, STATS_HEADS, 3], F32, name="stats")
 
-        def bias_and_squares(i, t):
-            q, squares, sumsq = q_of[i], squares_of[i], sumsq_of[i]
+        def add_bias(i, t):
+            q = q_of[i]
             nc.vector.tensor_tensor(
                 out=q[:, :, t, :],
                 in0=acc_of[i][t][:].rearrange("p (h d) -> p h d", h=HEADS),
                 in1=bias[:].rearrange("p (h d) -> p h d", h=HEADS),
                 op=ADD,
             )
-            for h in range(HEADS):
+
+        def sum_squares(i, t):
+            q, squares, sumsq = q_of[i], squares_of[i], sumsq_of[i]
+            for h in range(STATS_HEADS, HEADS):
                 nc.scalar.activation(
                     out=squares[:, t, h, :],
                     in_=q[:, h, t, :],
                     func=SQUARE,
-                    accum_out=sumsq[:, h, t : t + 1],
+                    accum_out=sumsq[:, t, h : h + 1],
                 )
+
+        def take_stats(i, t):
+            for h in range(0, STATS_HEADS, 2):
+                nc.vector.bn_stats(
+                    out=stats_of[i][:, t, h : h + 2, :].rearrange("p h s -> p (h s)"),
+                    in_=q_of[i][:, h : h + 2, t, :].rearrange("p h d -> p d h"),
+                )
+
+        def square_means(i):
+            msq = small.tile([P, MAX_TILES, STATS_HEADS], F32, name="msq")
+            nc.scalar.activation(
+                out=msq[:], in_=stats_of[i][:, :, :, 1], func=SQUARE, scale=8.0
+            )
+            msq_of[i] = msq
+
+        def add_deviations(i, engine):
+            engine.tensor_tensor(
+                out=sumsq_of[i][:, :, 0:STATS_HEADS],
+                in0=msq_of[i][:],
+                in1=stats_of[i][:, :, :, 2],
+                op=ADD,
+            )
 
         def invert_norms(i):
             tiles = blocks[i][2]
-            inverse = small.tile([P, HEADS, MAX_TILES], F32)
-            nc.scalar.activation(
-                out=inverse[:, :, 0:tiles], in_=sumsq_of[i][:, :, 0:tiles], func=RSQRT
-            )
+            inverse = small.tile([P, MAX_TILES, HEADS], F32)
+            nc.scalar.activation(out=inverse[:], in_=sumsq_of[i][:], func=RSQRT)
             inverse_of[i] = inverse
 
-        def apply_gain(i):
+        def apply_gain(i, engine):
             tiles = blocks[i][2]
-            factor = small.tile([P, HEADS, MAX_TILES], F32)
-            nc.vector.tensor_tensor(
-                out=factor[:, :, 0:tiles],
-                in0=inverse_of[i][:, :, 0:tiles],
-                in1=gain[:, 0:HEADS].unsqueeze(2).to_broadcast([P, HEADS, tiles]),
+            factor = small.tile([P, MAX_TILES, HEADS], F32)
+            engine.tensor_tensor(
+                out=factor[:],
+                in0=inverse_of[i][:],
+                in1=gain[:, 0:HEADS].unsqueeze(1).to_broadcast([P, MAX_TILES, HEADS]),
                 op=MULT,
             )
             factor_of[i] = factor
@@ -180,7 +205,8 @@ def tile_ufoattention_pb_kernel(tc, queries, Wq_words, Wq_scales, bq, gamma, out
                     engine.tensor_tensor(
                         out=q[:, h0:h1, 0:tiles, :],
                         in0=q[:, h0:h1, 0:tiles, :],
-                        in1=factor[:, h0:h1, 0:tiles]
+                        in1=factor[:, :, h0:h1]
+                        .rearrange("p t h -> p h t")
                         .unsqueeze(3)
                         .to_broadcast([P, h1 - h0, tiles, D_HEAD]),
                         op=MULT,
@@ -188,7 +214,7 @@ def tile_ufoattention_pb_kernel(tc, queries, Wq_words, Wq_scales, bq, gamma, out
             for h in range(by_vector, by_vector + by_scalar):
                 for t in range(tiles):
                     nc.scalar.activation(
-                        out=q[:, h, t, :], in_=q[:, h, t, :], func=COPY, scale=factor[:, h, t : t + 1]
+                        out=q[:, h, t, :], in_=q[:, h, t, :], func=COPY, scale=factor[:, t, h : h + 1]
                     )
             nc.sync.dma_start(
                 out=out[b, :, first : first + tiles * P, :].rearrange(
@@ -250,23 +276,36 @@ def tile_ufoattention_pb_kernel(tc, queries, Wq_words, Wq_scales, bq, gamma, out
 
         for i in range(n_blocks):
             tiles = blocks[i][2]
-            if i + 1 < n_blocks:
-                project_tiles(i + 1, ACC_BANKS - tiles)
             if i + 4 < n_blocks:
                 transpose_block(i + 4)
+            if i + 1 < n_blocks:
+                project_tiles(i + 1, ACC_BANKS - tiles)
             new_results(i)
-            for t in range(tiles):
-                bias_and_squares(i, t)
-                if i + 1 < n_blocks:
-                    project_tiles(i + 1, 1)
-            if i + 3 < n_blocks:
-                regroup_block(i + 3, nc.vector.tensor_copy)
-            invert_norms(i)
             if i >= 1:
-                apply_gain(i - 1)
+                square_means(i - 1)
+            if i >= 2:
+                invert_norms(i - 2)
+            if i + 3 < n_blocks:
+                regroup_block(i + 3, nc.scalar.copy)
+            for t in range(tiles):
+                add_bias(i, t)
+                sum_squares(i, t)
+            for t in range(tiles):
+                take_stats(i, t)
             if i + 2 < n_blocks:
                 quantise_block(i + 2)
+            if i >= 2:
+                apply_gain(i - 2, nc.vector)
+            if i >= 3:
+                scale_and_store(i - 3)
             if i >= 1:
-                scale_and_store(i - 1)
-        apply_gain(n_blocks - 1)
+                add_deviations(i - 1, nc.gpsimd)
+        square_means(n_blocks - 1)
+        scale_and_store(n_blocks - 3)
+        invert_norms(n_blocks - 2)
+        apply_gain(n_blocks - 2, nc.vector)
+        add_deviations(n_blocks - 1, nc.vector)
+        invert_norms(n_blocks - 1)
+        scale_and_store(n_blocks - 2)
+        apply_gain(n_blocks - 1, nc.vector)
         scale_and_store(n_blocks - 1)

@@ -281,29 +281,25 @@ def tile_ufoattention_pb_kernel(tc, queries, Wq_words, Wq_scales, bq, gamma, out
             if i + 1 < n_blocks:
                 project_tiles(i + 1, ACC_BANKS - tiles)
             new_results(i)
-            if i >= 1:
-                square_means(i - 1)
-            if i >= 2:
-                invert_norms(i - 2)
             if i + 3 < n_blocks:
                 regroup_block(i + 3, nc.scalar.copy)
             for t in range(tiles):
                 add_bias(i, t)
-                sum_squares(i, t)
             for t in range(tiles):
                 take_stats(i, t)
-            if i + 2 < n_blocks:
-                quantise_block(i + 2)
-            if i >= 2:
-                apply_gain(i - 2, nc.vector)
-            if i >= 3:
-                scale_and_store(i - 3)
             if i >= 1:
                 add_deviations(i - 1, nc.gpsimd)
-        square_means(n_blocks - 1)
-        scale_and_store(n_blocks - 3)
-        invert_norms(n_blocks - 2)
-        apply_gain(n_blocks - 2, nc.vector)
+            sum_squares(i, 0)
+            if i >= 1:
+                invert_norms(i - 1)
+            sum_squares(i, 1)
+            square_means(i)
+            if i + 2 < n_blocks:
+                quantise_block(i + 2)
+            if i >= 1:
+                apply_gain(i - 1, nc.vector)
+            if i >= 2:
+                scale_and_store(i - 2)
         add_deviations(n_blocks - 1, nc.vector)
         invert_norms(n_blocks - 1)
         scale_and_store(n_blocks - 2)

@@ -28,8 +28,6 @@ SPLIT = (0, 3)
 SPLIT_BEFORE_LAST = (5, 3)
 SPLIT_LAST = (5, 3)
 STATS_HEADS = 4
-PASSES = 2
-FIRST_REPEATED = 3
 GAIN_PAD = 32
 
 FLOPS = 2 * BATCH * TOKENS * D_IN * D_OUT
@@ -113,16 +111,15 @@ def tile_ufoattention_pb_kernel(tc, queries, Wq_words, Wq_scales, bq, gamma, out
             for t in range(len(acc_of[i]), min(len(acc_of[i]) + count, blocks[i][2])):
                 acc = psum_q.tile([P, D_OUT], F32, tag="acc")
                 tokens = slice(t * P, (t + 1) * P)
-                for rep in range(PASSES if i >= FIRST_REPEATED else 1):
-                    nc.tensor.matmul_mx(
-                        out=acc[:],
-                        lhsT=codes_of[i][:, tokens].bitcast(FP8X4),
-                        lhsT_scale=scales_of[i][:, tokens],
-                        rhs=w_words[:].bitcast(FP4X4),
-                        rhs_scale=w_scales[:],
-                        start=True,
-                        stop=True,
-                    )
+                nc.tensor.matmul_mx(
+                    out=acc[:],
+                    lhsT=codes_of[i][:, tokens].bitcast(FP8X4),
+                    lhsT_scale=scales_of[i][:, tokens],
+                    rhs=w_words[:].bitcast(FP4X4),
+                    rhs_scale=w_scales[:],
+                    start=True,
+                    stop=True,
+                )
                 acc_of[i].append(acc)
 
         def new_results(i):

@@ -24,9 +24,6 @@ WORDS = D_IN // 2
 SIZES = ((2, 2, 2, 2), (2, 2, 2, 2), (2, 2, 2, 2), (2, 2, 2, 2))
 MAX_TILES = 2
 ACC_BANKS = 4
-SPLIT = (0, 3)
-SPLIT_BEFORE_LAST = (5, 3)
-SPLIT_LAST = (5, 3)
 STATS_HEADS = 4
 GAIN_PAD = 32
 
@@ -48,9 +45,10 @@ def tile_ufoattention_pb_kernel(tc, queries, Wq_words, Wq_scales, bq, gamma, out
         ctx.enter_context(tc.manual_schedule())
         consts = ctx.enter_context(tc.tile_pool(name="consts", bufs=1))
         x_pool = ctx.enter_context(tc.tile_pool(name="x", bufs=n_blocks))
-        stage = ctx.enter_context(tc.tile_pool(name="stage", bufs=4))
-        results = ctx.enter_context(tc.tile_pool(name="results", bufs=8))
-        small = ctx.enter_context(tc.tile_pool(name="small", bufs=6))
+        stage = ctx.enter_context(tc.tile_pool(name="stage", bufs=n_blocks))
+        results = ctx.enter_context(tc.tile_pool(name="results", bufs=n_blocks))
+        small = ctx.enter_context(tc.tile_pool(name="small", bufs=n_blocks))
+        junk = ctx.enter_context(tc.tile_pool(name="junk", bufs=2))
         psum_t = ctx.enter_context(tc.psum_pool(name="psum_t", bufs=8 - ACC_BANKS))
         psum_q = ctx.enter_context(tc.psum_pool(name="psum_q", bufs=ACC_BANKS))
 
@@ -67,45 +65,38 @@ def tile_ufoattention_pb_kernel(tc, queries, Wq_words, Wq_scales, bq, gamma, out
             )
             x_of[i] = x_sb
 
-        def transpose_block(i):
-            tiles = blocks[i][2]
+        def transpose_tiles(i, t0, t1):
             words = x_of[i][:].rearrange("p t k -> p (t k)").bitcast(F32)
-            planes_of[i] = []
-            for t0 in range(0, tiles, 2):
-                planes = psum_t.tile([P, 2, 2, P], F32)
-                for j in range(min(2, tiles - t0)):
-                    first = (t0 + j) * WORDS
-                    for u in range(2):
-                        nc.tensor.transpose(
-                            planes[:, j, u, :], words[:, first + u : first + WORDS : 2], ident[:]
-                        )
-                planes_of[i].append(planes)
+            planes = psum_t.tile([P, MAX_TILES, 2, P], F32)
+            for t in range(t0, t1):
+                for u in range(2):
+                    nc.tensor.transpose(
+                        planes[:, t - t0, u, :],
+                        words[:, t * WORDS + u : (t + 1) * WORDS : 2],
+                        ident[:],
+                    )
+            planes_of[i, t0] = planes
 
-        def regroup_block(i, copy):
-            tiles = blocks[i][2]
-            grouped = stage.tile([P, MAX_TILES * D_IN], BF16, align_bytes=64)
-            grouped_words = grouped[:].bitcast(F32)
-            for t0 in range(0, tiles, 2):
-                n = min(2, tiles - t0)
-                copy(
-                    out=grouped_words[:, t0 * WORDS : (t0 + n) * WORDS].rearrange(
-                        "p (j r u) -> p j r u", j=n, u=2
-                    ),
-                    in_=planes_of[i][t0 // 2][:, 0:n, :, :].rearrange("p j u r -> p j r u"),
-                )
-            grouped_of[i] = grouped
-
-        def quantise_block(i):
-            tiles = blocks[i][2]
-            codes = stage.tile([P, MAX_TILES * P], U32, align_bytes=64)
-            scales = stage.tile([P, MAX_TILES * P], U8, align_bytes=64)
-            nc.vector.quantize_mx(
-                out=codes[:, 0 : tiles * P].bitcast(FP8X4),
-                scales=scales[:, 0 : tiles * P],
-                in_=grouped_of[i][:, 0 : tiles * D_IN],
+        def regroup_tiles(i, t0, t1, copy):
+            if t0 == 0:
+                grouped_of[i] = stage.tile([P, MAX_TILES * D_IN], BF16, align_bytes=64, name="grouped")
+            copy(
+                out=grouped_of[i][:]
+                .bitcast(F32)[:, t0 * WORDS : t1 * WORDS]
+                .rearrange("p (j r u) -> p j r u", j=t1 - t0, u=2),
+                in_=planes_of[i, t0][:, 0 : t1 - t0, :, :].rearrange("p j u r -> p j r u"),
             )
-            codes_of[i], scales_of[i] = codes, scales
-            acc_of[i] = []
+
+        def quantise_tiles(i, t0, t1):
+            if t0 == 0:
+                codes_of[i] = stage.tile([P, MAX_TILES * P], U32, align_bytes=64, name="codes")
+                scales_of[i] = stage.tile([P, MAX_TILES * P], U8, align_bytes=64, name="scales")
+                acc_of[i] = []
+            nc.vector.quantize_mx(
+                out=codes_of[i][:, t0 * P : t1 * P].bitcast(FP8X4),
+                scales=scales_of[i][:, t0 * P : t1 * P],
+                in_=grouped_of[i][:, t0 * D_IN : t1 * D_IN],
+            )
 
         def project_tiles(i, count):
             for t in range(len(acc_of[i]), min(len(acc_of[i]) + count, blocks[i][2])):
@@ -124,7 +115,7 @@ def tile_ufoattention_pb_kernel(tc, queries, Wq_words, Wq_scales, bq, gamma, out
 
         def new_results(i):
             q_of[i] = results.tile([P, HEADS, MAX_TILES, D_HEAD], F32, name="q")
-            squares_of[i] = stage.tile([P, MAX_TILES, HEADS, D_HEAD], F32, name="squares")
+            squares_of[i] = junk.tile([P, MAX_TILES, HEADS, D_HEAD], F32, name="squares")
             sumsq_of[i] = small.tile([P, MAX_TILES, HEADS], F32, name="sumsq")
             stats_of[i] = small.tile([P, MAX_TILES, STATS_HEADS, 3], F32, name="stats")
 
@@ -186,51 +177,50 @@ def tile_ufoattention_pb_kernel(tc, queries, Wq_words, Wq_scales, bq, gamma, out
             )
             factor_of[i] = factor
 
-        def scale_and_store(i):
-            b, first, tiles = blocks[i]
-            q, factor = q_of[i], factor_of[i]
-            by_vector, by_scalar = SPLIT
-            if i == n_blocks - 2:
-                by_vector, by_scalar = SPLIT_BEFORE_LAST
-            if i == n_blocks - 1:
-                by_vector, by_scalar = SPLIT_LAST
-            for engine, h0, h1 in (
-                (nc.vector, 0, by_vector),
-                (nc.gpsimd, by_vector + by_scalar, HEADS),
-            ):
-                if h1 > h0:
-                    engine.tensor_tensor(
-                        out=q[:, h0:h1, 0:tiles, :],
-                        in0=q[:, h0:h1, 0:tiles, :],
-                        in1=factor[:, :, h0:h1]
-                        .rearrange("p t h -> p h t")
-                        .unsqueeze(3)
-                        .to_broadcast([P, h1 - h0, tiles, D_HEAD]),
-                        op=MULT,
-                    )
-            for h in range(by_vector, by_vector + by_scalar):
-                for t in range(tiles):
+        def scale_tt(i, engine, h0, h1):
+            q = q_of[i]
+            engine.tensor_tensor(
+                out=q[:, h0:h1, :, :],
+                in0=q[:, h0:h1, :, :],
+                in1=factor_of[i][:, :, h0:h1]
+                .rearrange("p t h -> p h t")
+                .unsqueeze(3)
+                .to_broadcast([P, h1 - h0, MAX_TILES, D_HEAD]),
+                op=MULT,
+            )
+
+        def scale_act(i, h0, h1):
+            q = q_of[i]
+            for h in range(h0, h1):
+                for t in range(MAX_TILES):
                     nc.scalar.activation(
-                        out=q[:, h, t, :], in_=q[:, h, t, :], func=COPY, scale=factor[:, t, h : h + 1]
+                        out=q[:, h, t, :],
+                        in_=q[:, h, t, :],
+                        func=COPY,
+                        scale=factor_of[i][:, t, h : h + 1],
                     )
+
+        def store(i):
+            b, first, tiles = blocks[i]
             nc.sync.dma_start(
                 out=out[b, :, first : first + tiles * P, :].rearrange(
                     "h (p t) d -> p h (t d)", t=tiles
                 ),
-                in_=q[:, :, 0:tiles, :].rearrange("p h t d -> p h (t d)"),
+                in_=q_of[i][:, :, 0:tiles, :].rearrange("p h t d -> p h (t d)"),
             )
 
-        load_block(0)
-        w_words = consts.tile([P, 2 * D_OUT], U8, align_bytes=64)
-        nc.sync.dma_start(out=w_words[:].bitcast(I32), in_=Wq_words[0].bitcast(I32))
         w_scales = consts.tile([P, D_OUT], U8, align_bytes=64)
         nc.vector.memset(w_scales[:].bitcast(I32), 0)
+        load_block(0)
+        load_block(1)
         for quadrant in range(4):
             nc.sync.dma_start(
                 out=w_scales[32 * quadrant : 32 * quadrant + 4, :].bitcast(I32),
                 in_=Wq_scales[0, 4 * quadrant : 4 * quadrant + 4, :].bitcast(I32),
             )
-        for i in range(1, n_blocks):
+        w_words = consts.tile([P, 2 * D_OUT], U8, align_bytes=64)
+        nc.sync.dma_start(out=w_words[:].bitcast(I32), in_=Wq_words[0].bitcast(I32))
+        for i in range(2, n_blocks):
             load_block(i)
 
         ident = consts.tile([P, P], F32)
@@ -248,57 +238,75 @@ def tile_ufoattention_pb_kernel(tc, queries, Wq_words, Wq_scales, bq, gamma, out
         warm = consts.tile([P, 1], F32)
         nc.scalar.activation(out=warm[:], in_=one[:], func=RSQRT)
 
-        transpose_block(0)
-        regroup_block(0, nc.scalar.copy)
-
+        transpose_tiles(0, 0, 1)
+        regroup_tiles(0, 0, 1, nc.scalar.copy)
+        transpose_tiles(0, 1, 2)
+        regroup_tiles(0, 1, 2, nc.vector.tensor_copy)
         bias = consts.tile([P, D_OUT], F32)
         gain = consts.tile([P, GAIN_PAD], F32)
         bias_ps = psum_q.tile([P, D_OUT], F32, tag="acc")
         nc.tensor.matmul(out=bias_ps[:], lhsT=ones[:], rhs=row0[:, 0:D_OUT], start=True, stop=True)
-        nc.scalar.copy(out=bias[:], in_=bias_ps[:])
         gain_ps = psum_q.tile([P, D_OUT], F32, tag="acc")
         nc.tensor.matmul(
             out=gain_ps[:, 0:GAIN_PAD], lhsT=ones[:], rhs=row0[:, D_OUT:], start=True, stop=True
         )
-        nc.scalar.copy(out=gain[:], in_=gain_ps[:, 0:GAIN_PAD])
-
-        transpose_block(1)
-        regroup_block(1, nc.scalar.copy)
-        quantise_block(0)
-        transpose_block(2)
-        project_tiles(0, ACC_BANKS)
-        regroup_block(2, nc.scalar.copy)
-        quantise_block(1)
-        transpose_block(3)
+        transpose_tiles(1, 0, MAX_TILES)
+        regroup_tiles(1, 0, MAX_TILES, nc.scalar.copy)
+        quantise_tiles(0, 0, 1)
+        quantise_tiles(0, 1, 2)
+        nc.vector.tensor_copy(out=bias[:], in_=bias_ps[:])
+        nc.vector.tensor_copy(out=gain[:], in_=gain_ps[:, 0:GAIN_PAD])
+        project_tiles(0, 1)
+        transpose_tiles(2, 0, MAX_TILES)
+        project_tiles(0, 1)
+        regroup_tiles(2, 0, MAX_TILES, nc.scalar.copy)
+        transpose_tiles(3, 0, MAX_TILES)
 
         for i in range(n_blocks):
             tiles = blocks[i][2]
-            if i + 4 < n_blocks:
-                transpose_block(i + 4)
-            if i + 1 < n_blocks:
+            late = i + 3 >= n_blocks
+            s_heads = 5 if late else 3
+            if 1 <= i and i + 4 < n_blocks:
+                transpose_tiles(i + 4, 0, MAX_TILES)
+            if 1 <= i < n_blocks - 1:
                 project_tiles(i + 1, ACC_BANKS - tiles)
             new_results(i)
-            if i + 3 < n_blocks:
-                regroup_block(i + 3, nc.scalar.copy)
-            for t in range(tiles):
-                add_bias(i, t)
+            if late:
+                scale_act(i - 2, 0, s_heads)
+            elif i > 0:
+                regroup_tiles(i + 3, 0, MAX_TILES, nc.scalar.copy)
+            add_bias(i, 0)
+            if i == 0:
+                quantise_tiles(1, 0, MAX_TILES)
+                project_tiles(1, MAX_TILES)
+                transpose_tiles(4, 0, MAX_TILES)
+            add_bias(i, 1)
             for t in range(tiles):
                 take_stats(i, t)
             if i >= 1:
                 add_deviations(i - 1, nc.gpsimd)
             sum_squares(i, 0)
+            if i == 0:
+                regroup_tiles(3, 0, MAX_TILES, nc.scalar.copy)
             if i >= 1:
                 invert_norms(i - 1)
             sum_squares(i, 1)
             square_means(i)
-            if i + 2 < n_blocks:
-                quantise_block(i + 2)
             if i >= 1:
                 apply_gain(i - 1, nc.vector)
+            if i + 2 < n_blocks:
+                quantise_tiles(i + 2, 0, MAX_TILES)
             if i >= 2:
-                scale_and_store(i - 2)
+                scale_tt(i - 2, nc.gpsimd, s_heads, HEADS)
+                if not late:
+                    scale_act(i - 2, 0, s_heads)
+                store(i - 2)
+        scale_tt(n_blocks - 2, nc.vector, 0, 5)
+        scale_act(n_blocks - 2, 5, HEADS)
+        store(n_blocks - 2)
         add_deviations(n_blocks - 1, nc.vector)
         invert_norms(n_blocks - 1)
-        scale_and_store(n_blocks - 2)
         apply_gain(n_blocks - 1, nc.vector)
-        scale_and_store(n_blocks - 1)
+        scale_tt(n_blocks - 1, nc.vector, 0, 5)
+        scale_act(n_blocks - 1, 5, HEADS)
+        store(n_blocks - 1)

from contextlib import ExitStack

import concourse.mybir as mybir
from concourse.masks import make_identity

F32 = mybir.dt.float32
BF16 = mybir.dt.bfloat16
I32 = mybir.dt.int32
U32 = mybir.dt.uint32
U8 = mybir.dt.uint8
FP8X4 = mybir.dt.float8_e4m3fn_x4
FP4X4 = mybir.dt.float4_e2m1fn_x4
ADD = mybir.AluOpType.add
MULT = mybir.AluOpType.mult
SQUARE = mybir.ActivationFunctionType.Square
RSQRT = mybir.ActivationFunctionType.Abs_reciprocal_sqrt
COPY = mybir.ActivationFunctionType.Copy

P = 128
BATCH, TOKENS, D_IN = 4, 1024, 512
HEADS, D_HEAD = 8, 64
D_OUT = HEADS * D_HEAD
WORDS = D_IN // 2
SIZES = ((2, 2, 2, 2), (2, 2, 2, 2), (2, 2, 2, 2), (2, 2, 2, 2))
MAX_TILES = 2
ACC_BANKS = 4
STATS_HEADS = 4
GAIN_PAD = 32

FLOPS = 2 * BATCH * TOKENS * D_IN * D_OUT


def tile_ufoattention_pb_kernel(tc, queries, Wq_words, Wq_scales, bq, gamma, out):
    nc = tc.nc
    blocks = []
    for b in range(BATCH):
        first_token = 0
        for tiles in SIZES[b]:
            blocks.append((b, first_token, tiles))
            first_token += tiles * P
        assert first_token == TOKENS
    n_blocks = len(blocks)

    with ExitStack() as ctx:
        ctx.enter_context(tc.manual_schedule())
        consts = ctx.enter_context(tc.tile_pool(name="consts", bufs=1))
        x_pool = ctx.enter_context(tc.tile_pool(name="x", bufs=n_blocks))
        stage = ctx.enter_context(tc.tile_pool(name="stage", bufs=n_blocks))
        results = ctx.enter_context(tc.tile_pool(name="results", bufs=n_blocks))
        small = ctx.enter_context(tc.tile_pool(name="small", bufs=n_blocks))
        junk = ctx.enter_context(tc.tile_pool(name="junk", bufs=2))
        psum_t = ctx.enter_context(tc.psum_pool(name="psum_t", bufs=8 - ACC_BANKS))
        psum_q = ctx.enter_context(tc.psum_pool(name="psum_q", bufs=ACC_BANKS))

        x_of, planes_of, grouped_of, codes_of, scales_of = {}, {}, {}, {}, {}
        acc_of, q_of, squares_of, sumsq_of = {}, {}, {}, {}
        inverse_of, factor_of, stats_of, msq_of = {}, {}, {}, {}

        def load_block(i):
            b, first, tiles = blocks[i]
            x_sb = x_pool.tile([P, MAX_TILES, D_IN], BF16)
            rows = queries[b, first : first + tiles * P, :]
            nc.sync.dma_start(
                out=x_sb[:, 0:tiles, :], in_=rows.rearrange("(p t) k -> p t k", t=tiles)
            )
            x_of[i] = x_sb

        def transpose_tiles(i, t0, t1):
            words = x_of[i][:].rearrange("p t k -> p (t k)").bitcast(F32)
            planes = psum_t.tile([P, MAX_TILES, 2, P], F32)
            for t in range(t0, t1):
                for u in range(2):
                    nc.tensor.transpose(
                        planes[:, t - t0, u, :],
                        words[:, t * WORDS + u : (t + 1) * WORDS : 2],
                        ident[:],
                    )
            planes_of[i, t0] = planes

        def regroup_tiles(i, t0, t1, copy):
            if t0 == 0:
                grouped_of[i] = stage.tile([P, MAX_TILES * D_IN], BF16, align_bytes=64, name="grouped")
            copy(
                out=grouped_of[i][:]
                .bitcast(F32)[:, t0 * WORDS : t1 * WORDS]
                .rearrange("p (j r u) -> p j r u", j=t1 - t0, u=2),
                in_=planes_of[i, t0][:, 0 : t1 - t0, :, :].rearrange("p j u r -> p j r u"),
            )

        def quantise_tiles(i, t0, t1):
            if t0 == 0:
                codes_of[i] = stage.tile([P, MAX_TILES * P], U32, align_bytes=64, name="codes")
                scales_of[i] = stage.tile([P, MAX_TILES * P], U8, align_bytes=64, name="scales")
                acc_of[i] = []
            nc.vector.quantize_mx(
                out=codes_of[i][:, t0 * P : t1 * P].bitcast(FP8X4),
                scales=scales_of[i][:, t0 * P : t1 * P],
                in_=grouped_of[i][:, t0 * D_IN : t1 * D_IN],
            )

        def project_tiles(i, count):
            for t in range(len(acc_of[i]), min(len(acc_of[i]) + count, blocks[i][2])):
                acc = psum_q.tile([P, D_OUT], F32, tag="acc")
                tokens = slice(t * P, (t + 1) * P)
                nc.tensor.matmul_mx(
                    out=acc[:],
                    lhsT=codes_of[i][:, tokens].bitcast(FP8X4),
                    lhsT_scale=scales_of[i][:, tokens],
                    rhs=w_words[:].bitcast(FP4X4),
                    rhs_scale=w_scales[:],
                    start=True,
                    stop=True,
                )
                acc_of[i].append(acc)

        def new_results(i):
            q_of[i] = results.tile([P, HEADS, MAX_TILES, D_HEAD], F32, name="q")
            squares_of[i] = junk.tile([P, MAX_TILES, HEADS, D_HEAD], F32, name="squares")
            sumsq_of[i] = small.tile([P, MAX_TILES, HEADS], F32, name="sumsq")
            stats_of[i] = small.tile([P, MAX_TILES, STATS_HEADS, 3], F32, name="stats")

        def add_bias(i, t):
            q = q_of[i]
            nc.vector.tensor_tensor(
                out=q[:, :, t, :],
                in0=acc_of[i][t][:].rearrange("p (h d) -> p h d", h=HEADS),
                in1=bias[:].rearrange("p (h d) -> p h d", h=HEADS),
                op=ADD,
            )

        def sum_squares(i, t):
            q, squares, sumsq = q_of[i], squares_of[i], sumsq_of[i]
            for h in range(STATS_HEADS, HEADS):
                nc.scalar.activation(
                    out=squares[:, t, h, :],
                    in_=q[:, h, t, :],
                    func=SQUARE,
                    accum_out=sumsq[:, t, h : h + 1],
                )

        def take_stats(i, t):
            for h in range(0, STATS_HEADS, 2):
                nc.vector.bn_stats(
                    out=stats_of[i][:, t, h : h + 2, :].rearrange("p h s -> p (h s)"),
                    in_=q_of[i][:, h : h + 2, t, :].rearrange("p h d -> p d h"),
                )

        def square_means(i):
            msq = small.tile([P, MAX_TILES, STATS_HEADS], F32, name="msq")
            nc.scalar.activation(
                out=msq[:], in_=stats_of[i][:, :, :, 1], func=SQUARE, scale=8.0
            )
            msq_of[i] = msq

        def add_deviations(i, engine):
            engine.tensor_tensor(
                out=sumsq_of[i][:, :, 0:STATS_HEADS],
                in0=msq_of[i][:],
                in1=stats_of[i][:, :, :, 2],
                op=ADD,
            )

        def invert_norms(i):
            tiles = blocks[i][2]
            inverse = small.tile([P, MAX_TILES, HEADS], F32)
            nc.scalar.activation(out=inverse[:], in_=sumsq_of[i][:], func=RSQRT)
            inverse_of[i] = inverse

        def apply_gain(i, engine):
            tiles = blocks[i][2]
            factor = small.tile([P, MAX_TILES, HEADS], F32)
            engine.tensor_tensor(
                out=factor[:],
                in0=inverse_of[i][:],
                in1=gain[:, 0:HEADS].unsqueeze(1).to_broadcast([P, MAX_TILES, HEADS]),
                op=MULT,
            )
            factor_of[i] = factor

        def scale_tt(i, engine, h0, h1):
            q = q_of[i]
            engine.tensor_tensor(
                out=q[:, h0:h1, :, :],
                in0=q[:, h0:h1, :, :],
                in1=factor_of[i][:, :, h0:h1]
                .rearrange("p t h -> p h t")
                .unsqueeze(3)
                .to_broadcast([P, h1 - h0, MAX_TILES, D_HEAD]),
                op=MULT,
            )

        def scale_act(i, h0, h1):
            q = q_of[i]
            for h in range(h0, h1):
                for t in range(MAX_TILES):
                    nc.scalar.activation(
                        out=q[:, h, t, :],
                        in_=q[:, h, t, :],
                        func=COPY,
                        scale=factor_of[i][:, t, h : h + 1],
                    )

        def store(i):
            b, first, tiles = blocks[i]
            nc.sync.dma_start(
                out=out[b, :, first : first + tiles * P, :].rearrange(
                    "h (p t) d -> p h (t d)", t=tiles
                ),
                in_=q_of[i][:, :, 0:tiles, :].rearrange("p h t d -> p h (t d)"),
            )

        w_scales = consts.tile([P, D_OUT], U8, align_bytes=64)
        nc.vector.memset(w_scales[:].bitcast(I32), 0)
        load_block(0)
        load_block(1)
        for quadrant in range(4):
            nc.sync.dma_start(
                out=w_scales[32 * quadrant : 32 * quadrant + 4, :].bitcast(I32),
                in_=Wq_scales[0, 4 * quadrant : 4 * quadrant + 4, :].bitcast(I32),
            )
        w_words = consts.tile([P, 2 * D_OUT], U8, align_bytes=64)
        nc.sync.dma_start(out=w_words[:].bitcast(I32), in_=Wq_words[0].bitcast(I32))
        for i in range(2, n_blocks):
            load_block(i)

        ident = consts.tile([P, P], F32)
        make_identity(nc, ident[:])
        row0 = consts.tile([P, D_OUT + GAIN_PAD], BF16)
        nc.vector.memset(row0[:], 0.0)
        nc.scalar.dma_start(out=row0[0:1, 0:D_OUT], in_=bq.rearrange("(o n) -> o n", o=1))
        nc.scalar.dma_start(
            out=row0[0:1, D_OUT : D_OUT + HEADS], in_=gamma.rearrange("a h b c -> a (h b c)")
        )
        ones = consts.tile([P, P], BF16)
        nc.vector.memset(ones[:], 1.0)
        one = consts.tile([P, 1], F32)
        nc.vector.memset(one[:], 1.0)
        warm = consts.tile([P, 1], F32)
        nc.scalar.activation(out=warm[:], in_=one[:], func=RSQRT)

        transpose_tiles(0, 0, 1)
        regroup_tiles(0, 0, 1, nc.scalar.copy)
        transpose_tiles(0, 1, 2)
        regroup_tiles(0, 1, 2, nc.vector.tensor_copy)
        bias = consts.tile([P, D_OUT], F32)
        gain = consts.tile([P, GAIN_PAD], F32)
        bias_ps = psum_q.tile([P, D_OUT], F32, tag="acc")
        nc.tensor.matmul(out=bias_ps[:], lhsT=ones[:], rhs=row0[:, 0:D_OUT], start=True, stop=True)
        gain_ps = psum_q.tile([P, D_OUT], F32, tag="acc")
        nc.tensor.matmul(
            out=gain_ps[:, 0:GAIN_PAD], lhsT=ones[:], rhs=row0[:, D_OUT:], start=True, stop=True
        )
        transpose_tiles(1, 0, MAX_TILES)
        regroup_tiles(1, 0, MAX_TILES, nc.scalar.copy)
        quantise_tiles(0, 0, 1)
        quantise_tiles(0, 1, 2)
        nc.vector.tensor_copy(out=bias[:], in_=bias_ps[:])
        nc.vector.tensor_copy(out=gain[:], in_=gain_ps[:, 0:GAIN_PAD])
        project_tiles(0, 1)
        transpose_tiles(2, 0, MAX_TILES)
        project_tiles(0, 1)
        regroup_tiles(2, 0, MAX_TILES, nc.scalar.copy)
        transpose_tiles(3, 0, MAX_TILES)

        for i in range(n_blocks):
            tiles = blocks[i][2]
            late = i + 3 >= n_blocks
            s_heads = 5 if late else 3
            if 1 <= i and i + 4 < n_blocks:
                transpose_tiles(i + 4, 0, MAX_TILES)
            if 1 <= i < n_blocks - 1:
                project_tiles(i + 1, ACC_BANKS - tiles)
            new_results(i)
            if late:
                scale_act(i - 2, 0, s_heads)
            elif i > 0:
                regroup_tiles(i + 3, 0, MAX_TILES, nc.scalar.copy)
            add_bias(i, 0)
            if i == 0:
                quantise_tiles(1, 0, MAX_TILES)
                project_tiles(1, MAX_TILES)
                transpose_tiles(4, 0, MAX_TILES)
            add_bias(i, 1)
            for t in range(tiles):
                take_stats(i, t)
            if i >= 1:
                add_deviations(i - 1, nc.gpsimd)
            sum_squares(i, 0)
            if i == 0:
                regroup_tiles(3, 0, MAX_TILES, nc.scalar.copy)
            if i >= 1:
                invert_norms(i - 1)
            sum_squares(i, 1)
            square_means(i)
            if i >= 1:
                apply_gain(i - 1, nc.vector)
            if i + 2 < n_blocks:
                quantise_tiles(i + 2, 0, MAX_TILES)
            if i >= 2:
                scale_tt(i - 2, nc.gpsimd, s_heads, HEADS)
                if not late:
                    scale_act(i - 2, 0, s_heads)
                store(i - 2)
        scale_tt(n_blocks - 2, nc.vector, 0, 5)
        scale_act(n_blocks - 2, 5, HEADS)
        store(n_blocks - 2)
        add_deviations(n_blocks - 1, nc.vector)
        invert_norms(n_blocks - 1)
        apply_gain(n_blocks - 1, nc.vector)
        scale_tt(n_blocks - 1, nc.vector, 0, 5)
        scale_act(n_blocks - 1, 5, HEADS)
        store(n_blocks - 1)
